import numpy as np
import ml_dtypes


def mxq(x, axis, fmt="e4m3"):
    dtype, down = {"e4m3": (ml_dtypes.float8_e4m3fn, 7), "e5m2": (ml_dtypes.float8_e5m2, 14)}[fmt]
    v = np.moveaxis(np.asarray(x, np.float32).astype(ml_dtypes.bfloat16).astype(np.float64), axis, -1)
    blocks = v.reshape(v.shape[:-1] + (-1, 32))
    amax = np.abs(blocks).max(-1, keepdims=True)
    byte = np.maximum(np.where(amax > 0, np.frexp(amax)[1] - 1 + 127, 0) - down, 1)
    scale = np.exp2(byte - 127.0)
    codes = (blocks / scale).astype(np.float32).astype(dtype).astype(np.float64)
    return np.moveaxis((codes * scale).reshape(v.shape), -1, axis)


WIDE = False


def mx_kscale(k):
    if not WIDE:
        return np.ones(k)
    levels = np.array([10, -10, 5, -5, 0])
    if k % 512:
        return np.exp2(np.random.permutation(np.resize(levels, k // 32))).repeat(32)
    a = np.empty((k // 512, 16))
    for p in range(k // 512):
        a[p, :8] = np.random.permutation(np.resize(levels, 8))
        for g in range(8):
            far = levels[np.abs(levels - a[p, g]) >= 10]
            a[p, g + 8] = far[np.random.randint(len(far))]
    return np.exp2(a.ravel()).repeat(32)


BF16 = ml_dtypes.bfloat16


def bf(x):
    return np.asarray(x, np.float32).astype(BF16)


def f64(x):
    return np.asarray(x).astype(np.float64)


N, DIN, DOUT = 4096, 512, 128
C = 1.0


def sigmoid(v):
    return 1.0 / (1.0 + np.exp(-v))


def lorentz_points(gain, spread):
    t = 1.1 + gain * sigmoid(spread * np.random.standard_normal((N, 1)))
    u = np.random.standard_normal((N, DOUT - 1))
    u = u / np.sqrt(np.sum(u * u, axis=1, keepdims=True))
    return np.concatenate([t, u * np.sqrt(t * t - 1.0)], axis=1)


def setup_inputs():
    s = mx_kscale(N)
    q = lorentz_points(4.0, 0.4)
    q[:, :1] *= -1.0
    k = lorentz_points(4.0, 0.4)
    h = lorentz_points(10.0, 1.0)
    adj = (np.random.random((N, N)) < 0.01) * s[None, :]
    return {"q_neg": bf(q), "k": bf(k), "h": bf(h / s[:, None]), "adj": bf(adj),
            "att_bias": bf(7.0 + 0.2 * np.random.standard_normal(1)),
            "att_scale": bf(2.5 * (1.0 + 0.04 * np.random.standard_normal(1)))}


def reference(q_neg, k, h, adj, att_bias, att_scale):
    cin = f64(q_neg) @ f64(k).T
    att = f64(adj) * sigmoid((2.0 + 2.0 * cin) / f64(att_scale) + f64(att_bias))
    support = mxq(att, 1, "e4m3") @ mxq(f64(h), 0, "e4m3")
    l_inner = -support[:, :1] ** 2 + np.sum(support[:, 1:] ** 2, axis=-1, keepdims=True)
    denom = np.sqrt(np.maximum(np.abs(-l_inner), 1e-6)) / np.sqrt(C)
    return support / denom

@@ -1,0 +1,271 @@
+from contextlib import ExitStack
+
+import concourse.masks as masks
+import concourse.mybir as mybir
+
+F32 = mybir.dt.float32
+BF16 = mybir.dt.bfloat16
+U32 = mybir.dt.uint32
+U8 = mybir.dt.uint8
+FP8X4 = mybir.dt.float8_e4m3fn_x4
+FUNC = mybir.ActivationFunctionType
+ALU = mybir.AluOpType
+
+P = 128
+N = 4096
+D = 128
+PACK = 4
+K_PASS = P * PACK
+N_PASS = N // K_PASS
+N_BLOCKS = N // P
+
+PASSES_PER_UNIT = 2
+UNITS_PER_BLOCK = N_PASS // PASSES_PER_UNIT
+N_UNITS = N_BLOCKS * UNITS_PER_BLOCK
+UNIT_COLS = PASSES_PER_UNIT * P
+UNIT_VALS = UNIT_COLS * PACK
+UNIT_J = PASSES_PER_UNIT * K_PASS
+GROUP = 4
+
+SCORE_LEAD = 1
+MX_LAG = 5
+SCALE_LAG = 3
+ADJ_AHEAD = 4
+
+FLOPS = 2 * (2 * N * N * D)
+
+
+def tile_hybonetconv_pb_t_kernel(tc, q_neg, k, h, adj, att_bias, att_scale, out):
+    nc = tc.nc
+
+    q_view = q_neg.rearrange("(p b) d -> p b d", b=N_BLOCKS)
+    adj_view = adj.rearrange("(p b) j -> b p j", b=N_BLOCKS)
+    out_view = out.rearrange("(p b) d -> p b d", b=N_BLOCKS)
+    k_view = k.rearrange("(g p t) d -> p g (t d)", p=P, t=PACK)
+    h_view = h.rearrange("(g p t) d -> p g (t d)", p=P, t=PACK)
+
+    with ExitStack() as ctx:
+        const = ctx.enter_context(tc.tile_pool(name="const", bufs=1))
+        adj_pool = ctx.enter_context(tc.tile_pool(name="adj", bufs=ADJ_AHEAD + 1))
+        sig_pool = ctx.enter_context(tc.tile_pool(name="sig", bufs=4 + SCORE_LEAD))
+        att_pool = ctx.enter_context(tc.tile_pool(name="att", bufs=3))
+        mx_pool = ctx.enter_context(tc.tile_pool(name="mx", bufs=MX_LAG + 2))
+        norm_pool = ctx.enter_context(tc.tile_pool(name="norm", bufs=4))
+
+        h_sb = const.tile([P, N_PASS * PACK, D], BF16)
+        nc.sync.dma_start(out=h_sb[:].rearrange("p (g t) d -> p g (t d)", t=PACK), in_=h_view)
+        q_sb = const.tile([P, N_BLOCKS, D], BF16)
+        nc.sync.dma_start(out=q_sb[:, 0:GROUP, :], in_=q_view[:, 0:GROUP, :])
+        k_sb = const.tile([P, N_PASS * PACK, D], BF16)
+        k_passes = k_sb[:].rearrange("p (g t) d -> p g (t d)", t=PACK)
+
+        adj_tiles = {}
+        adj_tiles[0] = adj_pool.tile([P, N], BF16, name="adj_sb")
+        for quarter in range(UNITS_PER_BLOCK):
+            passes = slice(PASSES_PER_UNIT * quarter, PASSES_PER_UNIT * (quarter + 1))
+            nc.sync.dma_start(out=k_passes[:, passes, :], in_=k_view[:, passes, :])
+            cols = slice(UNIT_J * quarter, UNIT_J * (quarter + 1))
+            nc.sync.dma_start(out=adj_tiles[0][:, cols], in_=adj_view[0][:, cols])
+
+        def load_adj(b):
+            adj_sb = adj_pool.tile([P, N], BF16, name="adj_sb")
+            nc.sync.dma_start(out=adj_sb[:], in_=adj_view[b])
+            adj_tiles[b] = adj_sb
+
+        load_adj(1)
+        load_adj(2)
+        nc.sync.dma_start(out=q_sb[:, GROUP:N_BLOCKS, :], in_=q_view[:, GROUP:N_BLOCKS, :])
+        load_adj(3)
+
+        scale_bf = const.tile([P, 1], BF16)
+        nc.scalar.dma_start(out=scale_bf[:], in_=att_scale.partition_broadcast(P))
+        bias_bf = const.tile([P, 1], BF16)
+        nc.scalar.dma_start(out=bias_bf[:], in_=att_bias.partition_broadcast(P))
+
+        ident_bf = const.tile([P, P], BF16)
+        masks.make_identity(nc, ident_bf[:])
+        ident_f32 = const.tile([P, P], F32)
+        masks.make_identity(nc, ident_f32[:])
+        minus_half = const.tile([P, 1], F32)
+        nc.gpsimd.memset(minus_half[:], -0.5)
+
+        sig_scale = const.tile([P, 1], F32)
+        nc.vector.reciprocal(out=sig_scale[:], in_=scale_bf[:])
+        nc.vector.tensor_scalar_mul(out=sig_scale[:], in0=sig_scale[:], scalar1=2.0)
+        sig_bias = const.tile([P, 1], F32)
+        nc.vector.tensor_add(out=sig_bias[:], in0=sig_scale[:], in1=bias_bf[:])
+
+        h_grouped = const.tile([P, N_PASS, D, PACK], BF16, align_bytes=64)
+        nc.vector.tensor_copy(
+            out=h_grouped[:], in_=h_sb[:].rearrange("p (g t) d -> p g d t", t=PACK)
+        )
+        h_words = const.tile([P, N_PASS, D], U32, align_bytes=64)
+        h_scales = const.tile([P, N_PASS, D], U8, align_bytes=64)
+        nc.vector.quantize_mx(
+            out=h_words[:].rearrange("p g d -> p (g d)").bitcast(FP8X4),
+            scales=h_scales[:].rearrange("p g d -> p (g d)"),
+            in_=h_grouped[:].rearrange("p g d t -> p (g d t)"),
+        )
+
+        cin_ps = ctx.enter_context(tc.psum_pool(name="cin_ps", bufs=3))
+        adjT_ps = ctx.enter_context(tc.psum_pool(name="adjT_ps", bufs=3))
+        sup_ps = ctx.enter_context(tc.psum_pool(name="sup_ps", bufs=2))
+
+        qT = const.tile([P, N_BLOCKS, P], BF16)
+        kT = const.tile([P, N_PASS * PACK, P], BF16)
+
+        def turn(src, dst, first):
+            turned = cin_ps.tile([P, GROUP, P], BF16, name="turned", tag="cin")
+            for n in range(GROUP):
+                nc.tensor.transpose(turned[:, n, :], src[:, first + n, :], ident_bf[:])
+            nc.scalar.copy(out=dst[:, first : first + GROUP, :], in_=turned[:])
+
+        adjT_tiles = {}
+        cin_tiles = {}
+        sig_tiles = {}
+        att_tiles = {}
+        word_tiles = {}
+        plane_tiles = {}
+        support_tiles = {}
+        rnorm_tiles = {}
+
+        def transpose_adj(s):
+            b, quarter = divmod(s, UNITS_PER_BLOCK)
+            adj_words = adj_tiles[b][:].bitcast(F32)
+            adjT = adjT_ps.tile([P, 2, PASSES_PER_UNIT, P], F32, name="adjT")
+            for gg in range(PASSES_PER_UNIT):
+                for u in range(2):
+                    first = 2 * P * (PASSES_PER_UNIT * quarter + gg)
+                    nc.tensor.transpose(
+                        adjT[:, u, gg, :], adj_words[:, first + u : first + 2 * P : 2], ident_f32[:]
+                    )
+            adjT_tiles[s] = adjT
+
+        def scores(s, gg):
+            b, quarter = divmod(s, UNITS_PER_BLOCK)
+            g = PASSES_PER_UNIT * quarter + gg
+            cin = cin_ps.tile([P, PACK, P], F32, name="cin", tag="cin")
+            for t in range(PACK):
+                nc.tensor.matmul(
+                    out=cin[:, t, :],
+                    lhsT=kT[:, PACK * g + t, :],
+                    rhs=qT[:, b, :],
+                    start=True,
+                    stop=True,
+                )
+            cin_tiles[(s, gg)] = cin
+
+        def sigmoid(s):
+            sig = sig_pool.tile([P, UNIT_VALS], F32, name="sig")
+            for gg in range(PASSES_PER_UNIT):
+                nc.scalar.activation(
+                    out=sig[:, gg * K_PASS : (gg + 1) * K_PASS].rearrange(
+                        "p (i t) -> p i t", t=PACK
+                    ),
+                    in_=cin_tiles[(s, gg)][:].rearrange("p t i -> p i t"),
+                    func=FUNC.Sigmoid,
+                    bias=sig_bias[:],
+                    scale=sig_scale[:],
+                )
+            sig_tiles[s] = sig
+
+        def weigh(s):
+            att = att_pool.tile([P, UNIT_VALS], BF16, name="att", align_bytes=64)
+            adjT_bf = adjT_tiles[s][:].rearrange("p u gg i -> p (u gg i)").bitcast(BF16)
+            nc.vector.tensor_tensor(
+                out=att[:].rearrange("p (c u e) -> p c u e", u=2, e=2),
+                in0=sig_tiles[s][:].rearrange("p (c u e) -> p c u e", u=2, e=2),
+                in1=adjT_bf.rearrange("p (u c e) -> p c u e", u=2, e=2),
+                op=ALU.mult,
+            )
+            att_tiles[s] = att
+
+        def quantise(s):
+            words = mx_pool.tile([P, UNIT_COLS], U32, name="words", align_bytes=64)
+            planes = mx_pool.tile([P, UNIT_COLS], U8, name="planes", align_bytes=64)
+            nc.vector.quantize_mx(
+                out=words[:].bitcast(FP8X4), scales=planes[:], in_=att_tiles[s][:]
+            )
+            word_tiles[s] = words
+            plane_tiles[s] = planes
+
+        def aggregate(s):
+            b, quarter = divmod(s, UNITS_PER_BLOCK)
+            if quarter == 0:
+                support_tiles[b] = sup_ps.tile([P, D], F32, name="support")
+            words = word_tiles[s]
+            planes = plane_tiles[s]
+            for gg in range(PASSES_PER_UNIT):
+                g = PASSES_PER_UNIT * quarter + gg
+                cols = slice(gg * P, (gg + 1) * P)
+                nc.tensor.matmul_mx(
+                    out=support_tiles[b][:],
+                    lhsT=words[:, cols].bitcast(FP8X4),
+                    lhsT_scale=planes[:, cols],
+                    rhs=h_words[:, g, :].bitcast(FP8X4),
+                    rhs_scale=h_scales[:, g, :],
+                    start=(g == 0),
+                    stop=(g == N_PASS - 1),
+                )
+
+        def norms(b):
+            support = support_tiles[b]
+            squares = norm_pool.tile([P, D], F32, name="squares")
+            total = norm_pool.tile([P, 1], F32, name="total")
+            nc.scalar.activation(
+                out=squares[:], in_=support[:], func=FUNC.Square, accum_out=total[:]
+            )
+            lorentz = norm_pool.tile([P, 1], F32, name="lorentz")
+            nc.gpsimd.tensor_scalar(
+                out=lorentz[:], in0=squares[:, 0:1], scalar1=-2.0, scalar2=total[:], op0=ALU.mult, op1=ALU.add
+            )
+            size = norm_pool.tile([P, 1], F32, name="size")
+            nc.gpsimd.tensor_scalar(
+                out=size[:], in0=lorentz[:], scalar1=-1.0, scalar2=lorentz[:], op0=ALU.mult, op1=ALU.max
+            )
+            floored = norm_pool.tile([P, 1], F32, name="floored")
+            nc.gpsimd.tensor_scalar(
+                out=floored[:], in0=size[:], scalar1=1e-6, scalar2=None, op0=ALU.max
+            )
+            rnorm = norm_pool.tile([P, 1], F32, name="rnorm")
+            nc.gpsimd.tensor_tensor(out=rnorm[:], in0=floored[:], in1=minus_half[:], op=ALU.pow)
+            rnorm_tiles[b] = rnorm
+
+        def scale_and_store(b):
+            result = norm_pool.tile([P, D], F32, name="result")
+            nc.scalar.activation(
+                out=result[:], in_=support_tiles[b][:], func=FUNC.Copy, scale=rnorm_tiles[b][:]
+            )
+            nc.sync.dma_start(out=out_view[:, b, :], in_=result[:])
+
+        with tc.manual_schedule():
+            for step in range(-SCORE_LEAD, N_UNITS + MX_LAG + SCALE_LAG):
+                ahead = step + SCORE_LEAD
+                if 0 <= step < N_UNITS:
+                    b, quarter = divmod(step, UNITS_PER_BLOCK)
+                    if quarter == 0 and b + ADJ_AHEAD < N_BLOCKS:
+                        load_adj(b + ADJ_AHEAD)
+                    transpose_adj(step)
+                if ahead < N_UNITS:
+                    b_ahead, quarter_ahead = divmod(ahead, UNITS_PER_BLOCK)
+                    if quarter_ahead == 0 and b_ahead % GROUP == 0:
+                        turn(q_sb, qT, b_ahead)
+                    if b_ahead == 0:
+                        for gg in range(PASSES_PER_UNIT):
+                            turn(k_sb, kT, PACK * (PASSES_PER_UNIT * quarter_ahead + gg))
+                    scores(ahead, 0)
+                if 0 <= step - MX_LAG < N_UNITS:
+                    aggregate(step - MX_LAG)
+                if ahead < N_UNITS:
+                    scores(ahead, 1)
+                    sigmoid(ahead)
+                if 0 <= step < N_UNITS:
+                    weigh(step)
+                if 0 <= step - 1 < N_UNITS:
+                    quantise(step - 1)
+                closed, rest = divmod(step - MX_LAG + 1, UNITS_PER_BLOCK)
+                if rest == 0 and 1 <= closed <= N_BLOCKS:
+                    norms(closed - 1)
+                scaled, rest = divmod(step - MX_LAG - SCALE_LAG + 1, UNITS_PER_BLOCK)
+                if rest == 0 and 1 <= scaled <= N_BLOCKS:
+                    scale_and_store(scaled - 1)

@@ -27,6 +27,9 @@ UNIT_VALS = UNIT_COLS * PACK
 UNIT_J = PASSES_PER_UNIT * K_PASS
 GROUP = 4
 
+GPSIMD_QUARTER = 1
+GPSIMD_LAG = 2
+
 SCORE_LEAD = 1
 MX_LAG = 5
 SCALE_LAG = 3
@@ -47,9 +50,10 @@ def tile_hybonetconv_pb_t_kernel(tc, q_neg, k, h, adj, att_bias, att_scale, out)
     with ExitStack() as ctx:
         const = ctx.enter_context(tc.tile_pool(name="const", bufs=1))
         adj_pool = ctx.enter_context(tc.tile_pool(name="adj", bufs=ADJ_AHEAD + 1))
-        sig_pool = ctx.enter_context(tc.tile_pool(name="sig", bufs=4 + SCORE_LEAD))
+        sig_pool = ctx.enter_context(tc.tile_pool(name="sig", bufs=6 + SCORE_LEAD))
         att_pool = ctx.enter_context(tc.tile_pool(name="att", bufs=3))
         mx_pool = ctx.enter_context(tc.tile_pool(name="mx", bufs=MX_LAG + 2))
+        side_pool = ctx.enter_context(tc.tile_pool(name="side", bufs=2))
         norm_pool = ctx.enter_context(tc.tile_pool(name="norm", bufs=4))
 
         h_sb = const.tile([P, N_PASS * PACK, D], BF16)
@@ -180,6 +184,28 @@ def tile_hybonetconv_pb_t_kernel(tc, q_neg, k, h, adj, att_bias, att_scale, out)
             )
             att_tiles[s] = att
 
+        def weigh_on_gpsimd(s):
+            adjS = side_pool.tile([P, 2, UNIT_COLS], F32, name="adjS")
+            nc.vector.tensor_copy(
+                out=adjS[:], in_=adjT_tiles[s][:].rearrange("p u gg i -> p u (gg i)")
+            )
+            att = side_pool.tile([P, UNIT_VALS], BF16, name="att_side", align_bytes=64)
+            att_view = att[:].rearrange("p (c u e) -> p c u e", u=2, e=2)
+            sig_view = sig_tiles[s][:].rearrange("p (c u e) -> p c u e", u=2, e=2)
+            adj_view_bf = (
+                adjS[:].rearrange("p u c -> p (u c)").bitcast(BF16)
+                .rearrange("p (u c e) -> p c u e", u=2, e=2)
+            )
+            for gg in range(PASSES_PER_UNIT):
+                cols = slice(gg * P, (gg + 1) * P)
+                nc.gpsimd.tensor_tensor(
+                    out=att_view[:, cols, :, :],
+                    in0=sig_view[:, cols, :, :],
+                    in1=adj_view_bf[:, cols, :, :],
+                    op=ALU.mult,
+                )
+            att_tiles[s] = att
+
         def quantise(s):
             words = mx_pool.tile([P, UNIT_COLS], U32, name="words", align_bytes=64)
             planes = mx_pool.tile([P, UNIT_COLS], U8, name="planes", align_bytes=64)
@@ -260,9 +286,15 @@ def tile_hybonetconv_pb_t_kernel(tc, q_neg, k, h, adj, att_bias, att_scale, out)
                     scores(ahead, 1)
                     sigmoid(ahead)
                 if 0 <= step < N_UNITS:
-                    weigh(step)
-                if 0 <= step - 1 < N_UNITS:
+                    if step % UNITS_PER_BLOCK == GPSIMD_QUARTER:
+                        weigh_on_gpsimd(step)
+                    else:
+                        weigh(step)
+                if 0 <= step - 1 < N_UNITS and (step - 1) % UNITS_PER_BLOCK != GPSIMD_QUARTER:
                     quantise(step - 1)
+                slow = step - GPSIMD_LAG
+                if 0 <= slow < N_UNITS and slow % UNITS_PER_BLOCK == GPSIMD_QUARTER:
+                    quantise(slow)
                 closed, rest = divmod(step - MX_LAG + 1, UNITS_PER_BLOCK)
                 if rest == 0 and 1 <= closed <= N_BLOCKS:
                     norms(closed - 1)

@@ -27,11 +27,10 @@ UNIT_VALS = UNIT_COLS * PACK
 UNIT_J = PASSES_PER_UNIT * K_PASS
 GROUP = 4
 
-GPSIMD_QUARTER = 1
-GPSIMD_LAG = 2
+GPSIMD_QUARTER = 0
 
 SCORE_LEAD = 1
-MX_LAG = 5
+MX_LAG = 6
 SCALE_LAG = 3
 ADJ_AHEAD = 4
 
@@ -52,7 +51,7 @@ def tile_hybonetconv_pb_t_kernel(tc, q_neg, k, h, adj, att_bias, att_scale, out)
         adj_pool = ctx.enter_context(tc.tile_pool(name="adj", bufs=ADJ_AHEAD + 1))
         sig_pool = ctx.enter_context(tc.tile_pool(name="sig", bufs=6 + SCORE_LEAD))
         att_pool = ctx.enter_context(tc.tile_pool(name="att", bufs=3))
-        mx_pool = ctx.enter_context(tc.tile_pool(name="mx", bufs=MX_LAG + 2))
+        mx_pool = ctx.enter_context(tc.tile_pool(name="mx", bufs=3))
         side_pool = ctx.enter_context(tc.tile_pool(name="side", bufs=2))
         norm_pool = ctx.enter_context(tc.tile_pool(name="norm", bufs=4))
 
@@ -173,24 +172,27 @@ def tile_hybonetconv_pb_t_kernel(tc, q_neg, k, h, adj, att_bias, att_scale, out)
                 )
             sig_tiles[s] = sig
 
+        def att_of(s):
+            b, quarter = divmod(s, UNITS_PER_BLOCK)
+            if b not in att_tiles:
+                att_tiles[b] = att_pool.tile([P, UNITS_PER_BLOCK * UNIT_VALS], BF16, name="att", align_bytes=64)
+            return att_tiles[b][:, quarter * UNIT_VALS : (quarter + 1) * UNIT_VALS]
+
         def weigh(s):
-            att = att_pool.tile([P, UNIT_VALS], BF16, name="att", align_bytes=64)
             adjT_bf = adjT_tiles[s][:].rearrange("p u gg i -> p (u gg i)").bitcast(BF16)
             nc.vector.tensor_tensor(
-                out=att[:].rearrange("p (c u e) -> p c u e", u=2, e=2),
+                out=att_of(s).rearrange("p (c u e) -> p c u e", u=2, e=2),
                 in0=sig_tiles[s][:].rearrange("p (c u e) -> p c u e", u=2, e=2),
                 in1=adjT_bf.rearrange("p (u c e) -> p c u e", u=2, e=2),
                 op=ALU.mult,
             )
-            att_tiles[s] = att
 
         def weigh_on_gpsimd(s):
             adjS = side_pool.tile([P, 2, UNIT_COLS], F32, name="adjS")
             nc.vector.tensor_copy(
                 out=adjS[:], in_=adjT_tiles[s][:].rearrange("p u gg i -> p u (gg i)")
             )
-            att = side_pool.tile([P, UNIT_VALS], BF16, name="att_side", align_bytes=64)
-            att_view = att[:].rearrange("p (c u e) -> p c u e", u=2, e=2)
+            att_view = att_of(s).rearrange("p (c u e) -> p c u e", u=2, e=2)
             sig_view = sig_tiles[s][:].rearrange("p (c u e) -> p c u e", u=2, e=2)
             adj_view_bf = (
                 adjS[:].rearrange("p u c -> p (u c)").bitcast(BF16)
@@ -204,26 +206,25 @@ def tile_hybonetconv_pb_t_kernel(tc, q_neg, k, h, adj, att_bias, att_scale, out)
                     in1=adj_view_bf[:, cols, :, :],
                     op=ALU.mult,
                 )
-            att_tiles[s] = att
 
-        def quantise(s):
-            words = mx_pool.tile([P, UNIT_COLS], U32, name="words", align_bytes=64)
-            planes = mx_pool.tile([P, UNIT_COLS], U8, name="planes", align_bytes=64)
+        def quantise(b):
+            words = mx_pool.tile([P, N_PASS * P], U32, name="words", align_bytes=64)
+            planes = mx_pool.tile([P, N_PASS * P], U8, name="planes", align_bytes=64)
             nc.vector.quantize_mx(
-                out=words[:].bitcast(FP8X4), scales=planes[:], in_=att_tiles[s][:]
+                out=words[:].bitcast(FP8X4), scales=planes[:], in_=att_tiles[b][:]
             )
-            word_tiles[s] = words
-            plane_tiles[s] = planes
+            word_tiles[b] = words
+            plane_tiles[b] = planes
 
         def aggregate(s):
             b, quarter = divmod(s, UNITS_PER_BLOCK)
             if quarter == 0:
                 support_tiles[b] = sup_ps.tile([P, D], F32, name="support")
-            words = word_tiles[s]
-            planes = plane_tiles[s]
+            words = word_tiles[b]
+            planes = plane_tiles[b]
             for gg in range(PASSES_PER_UNIT):
                 g = PASSES_PER_UNIT * quarter + gg
-                cols = slice(gg * P, (gg + 1) * P)
+                cols = slice(g * P, (g + 1) * P)
                 nc.tensor.matmul_mx(
                     out=support_tiles[b][:],
                     lhsT=words[:, cols].bitcast(FP8X4),
@@ -290,11 +291,9 @@ def tile_hybonetconv_pb_t_kernel(tc, q_neg, k, h, adj, att_bias, att_scale, out)
                         weigh_on_gpsimd(step)
                     else:
                         weigh(step)
-                if 0 <= step - 1 < N_UNITS and (step - 1) % UNITS_PER_BLOCK != GPSIMD_QUARTER:
-                    quantise(step - 1)
-                slow = step - GPSIMD_LAG
-                if 0 <= slow < N_UNITS and slow % UNITS_PER_BLOCK == GPSIMD_QUARTER:
-                    quantise(slow)
+                done, rest = divmod(step, UNITS_PER_BLOCK)
+                if rest == 0 and 1 <= done <= N_BLOCKS:
+                    quantise(done - 1)
                 closed, rest = divmod(step - MX_LAG + 1, UNITS_PER_BLOCK)
                 if rest == 0 and 1 <= closed <= N_BLOCKS:
                     norms(closed - 1)

@@ -188,22 +188,17 @@ def tile_hybonetconv_pb_t_kernel(tc, q_neg, k, h, adj, att_bias, att_scale, out)
             )
 
         def weigh_on_gpsimd(s):
-            adjS = side_pool.tile([P, 2, UNIT_COLS], F32, name="adjS")
+            adjS = side_pool.tile([P, UNIT_COLS, 2], F32, name="adjS")
             nc.vector.tensor_copy(
-                out=adjS[:], in_=adjT_tiles[s][:].rearrange("p u gg i -> p u (gg i)")
+                out=adjS[:], in_=adjT_tiles[s][:].rearrange("p u gg i -> p (gg i) u")
             )
-            att_view = att_of(s).rearrange("p (c u e) -> p c u e", u=2, e=2)
-            sig_view = sig_tiles[s][:].rearrange("p (c u e) -> p c u e", u=2, e=2)
-            adj_view_bf = (
-                adjS[:].rearrange("p u c -> p (u c)").bitcast(BF16)
-                .rearrange("p (u c e) -> p c u e", u=2, e=2)
-            )
+            adjS_bf = adjS[:].rearrange("p c u -> p (c u)").bitcast(BF16)
             for gg in range(PASSES_PER_UNIT):
-                cols = slice(gg * P, (gg + 1) * P)
+                vals = slice(gg * K_PASS, (gg + 1) * K_PASS)
                 nc.gpsimd.tensor_tensor(
-                    out=att_view[:, cols, :, :],
-                    in0=sig_view[:, cols, :, :],
-                    in1=adj_view_bf[:, cols, :, :],
+                    out=att_of(s)[:, vals],
+                    in0=sig_tiles[s][:, vals],
+                    in1=adjS_bf[:, vals],
                     op=ALU.mult,
                 )
 

@@ -32,6 +32,12 @@ GPSIMD_QUARTER = 0
 SCORE_LEAD = 1
 MX_LAG = 6
 SCALE_LAG = 3
+NORM_BATCH = 4
+BATCHES = [list(range(b, b + NORM_BATCH)) for b in range(0, N_BLOCKS - NORM_BATCH, NORM_BATCH)] + [
+    [N_BLOCKS - 4, N_BLOCKS - 3],
+    [N_BLOCKS - 2],
+    [N_BLOCKS - 1],
+]
 ADJ_AHEAD = 4
 
 FLOPS = 2 * (2 * N * N * D)
@@ -53,7 +59,8 @@ def tile_hybonetconv_pb_t_kernel(tc, q_neg, k, h, adj, att_bias, att_scale, out)
         att_pool = ctx.enter_context(tc.tile_pool(name="att", bufs=3))
         mx_pool = ctx.enter_context(tc.tile_pool(name="mx", bufs=3))
         side_pool = ctx.enter_context(tc.tile_pool(name="side", bufs=2))
-        norm_pool = ctx.enter_context(tc.tile_pool(name="norm", bufs=4))
+        norm_pool = ctx.enter_context(tc.tile_pool(name="norm", bufs=2))
+        result_pool = ctx.enter_context(tc.tile_pool(name="result", bufs=4))
 
         h_sb = const.tile([P, N_PASS * PACK, D], BF16)
         nc.sync.dma_start(out=h_sb[:].rearrange("p (g t) d -> p g (t d)", t=PACK), in_=h_view)
@@ -89,7 +96,7 @@ def tile_hybonetconv_pb_t_kernel(tc, q_neg, k, h, adj, att_bias, att_scale, out)
         masks.make_identity(nc, ident_bf[:])
         ident_f32 = const.tile([P, P], F32)
         masks.make_identity(nc, ident_f32[:])
-        minus_half = const.tile([P, 1], F32)
+        minus_half = const.tile([P, NORM_BATCH], F32)
         nc.gpsimd.memset(minus_half[:], -0.5)
 
         sig_scale = const.tile([P, 1], F32)
@@ -130,7 +137,11 @@ def tile_hybonetconv_pb_t_kernel(tc, q_neg, k, h, adj, att_bias, att_scale, out)
         word_tiles = {}
         plane_tiles = {}
         support_tiles = {}
-        rnorm_tiles = {}
+        squares_tiles = {}
+        total_tiles = {}
+        support_sb_tiles = {}
+        floored_tiles = {}
+        batch_of = {b: (batch, j) for batch, blocks in enumerate(BATCHES) for j, b in enumerate(blocks)}
 
         def transpose_adj(s):
             b, quarter = divmod(s, UNITS_PER_BLOCK)
@@ -230,35 +241,58 @@ def tile_hybonetconv_pb_t_kernel(tc, q_neg, k, h, adj, att_bias, att_scale, out)
                     stop=(g == N_PASS - 1),
                 )
 
-        def norms(b):
-            support = support_tiles[b]
-            squares = norm_pool.tile([P, D], F32, name="squares")
-            total = norm_pool.tile([P, 1], F32, name="total")
+        def empty(b):
+            batch, j = batch_of[b]
+            if j == 0:
+                squares_tiles[batch] = norm_pool.tile([P, NORM_BATCH, D], F32, name="squares")
+                total_tiles[batch] = norm_pool.tile([P, NORM_BATCH], F32, name="total")
+                support_sb_tiles[batch] = norm_pool.tile([P, NORM_BATCH, D], F32, name="support_sb")
             nc.scalar.activation(
-                out=squares[:], in_=support[:], func=FUNC.Square, accum_out=total[:]
+                out=squares_tiles[batch][:, j, :],
+                in_=support_tiles[b][:],
+                func=FUNC.Square,
+                accum_out=total_tiles[batch][:, j : j + 1],
             )
-            lorentz = norm_pool.tile([P, 1], F32, name="lorentz")
-            nc.gpsimd.tensor_scalar(
-                out=lorentz[:], in0=squares[:, 0:1], scalar1=-2.0, scalar2=total[:], op0=ALU.mult, op1=ALU.add
-            )
-            size = norm_pool.tile([P, 1], F32, name="size")
-            nc.gpsimd.tensor_scalar(
-                out=size[:], in0=lorentz[:], scalar1=-1.0, scalar2=lorentz[:], op0=ALU.mult, op1=ALU.max
-            )
-            floored = norm_pool.tile([P, 1], F32, name="floored")
-            nc.gpsimd.tensor_scalar(
-                out=floored[:], in0=size[:], scalar1=1e-6, scalar2=None, op0=ALU.max
-            )
-            rnorm = norm_pool.tile([P, 1], F32, name="rnorm")
-            nc.gpsimd.tensor_tensor(out=rnorm[:], in0=floored[:], in1=minus_half[:], op=ALU.pow)
-            rnorm_tiles[b] = rnorm
+            nc.scalar.copy(out=support_sb_tiles[batch][:, j, :], in_=support_tiles[b][:])
 
-        def scale_and_store(b):
-            result = norm_pool.tile([P, D], F32, name="result")
-            nc.scalar.activation(
-                out=result[:], in_=support_tiles[b][:], func=FUNC.Copy, scale=rnorm_tiles[b][:]
+        def sizes(batch):
+            n = len(BATCHES[batch])
+            lorentz = norm_pool.tile([P, NORM_BATCH], F32, name="lorentz")
+            nc.vector.scalar_tensor_tensor(
+                out=lorentz[:, 0:n],
+                in0=squares_tiles[batch][:, 0:n, 0],
+                scalar=-2.0,
+                in1=total_tiles[batch][:, 0:n],
+                op0=ALU.mult,
+                op1=ALU.add,
             )
-            nc.sync.dma_start(out=out_view[:, b, :], in_=result[:])
+            size = norm_pool.tile([P, NORM_BATCH], F32, name="size")
+            nc.vector.scalar_tensor_tensor(
+                out=size[:, 0:n], in0=lorentz[:, 0:n], scalar=-1.0, in1=lorentz[:, 0:n], op0=ALU.mult, op1=ALU.max
+            )
+            floored = norm_pool.tile([P, NORM_BATCH], F32, name="floored")
+            nc.vector.tensor_scalar(
+                out=floored[:, 0:n], in0=size[:, 0:n], scalar1=1e-6, scalar2=None, op0=ALU.max
+            )
+            floored_tiles[batch] = floored
+
+        def scale_and_store(batch):
+            n = len(BATCHES[batch])
+            rnorm = norm_pool.tile([P, NORM_BATCH], F32, name="rnorm")
+            nc.gpsimd.tensor_tensor(
+                out=rnorm[:, 0:n], in0=floored_tiles[batch][:, 0:n], in1=minus_half[:, 0:n], op=ALU.pow
+            )
+            for j, b in enumerate(BATCHES[batch]):
+                result = result_pool.tile([P, D], F32, name="result")
+                nc.gpsimd.tensor_scalar(
+                    out=result[:],
+                    in0=support_sb_tiles[batch][:, j, :],
+                    scalar1=rnorm[:, j : j + 1],
+                    scalar2=0.0,
+                    op0=ALU.mult,
+                    op1=ALU.add,
+                )
+                nc.sync.dma_start(out=out_view[:, b, :], in_=result[:])
 
         with tc.manual_schedule():
             for step in range(-SCORE_LEAD, N_UNITS + MX_LAG + SCALE_LAG):
@@ -281,17 +315,21 @@ def tile_hybonetconv_pb_t_kernel(tc, q_neg, k, h, adj, att_bias, att_scale, out)
                 if ahead < N_UNITS:
                     scores(ahead, 1)
                     sigmoid(ahead)
+                scaled, rest = divmod(step - MX_LAG - SCALE_LAG + 1, UNITS_PER_BLOCK)
+                scaled = scaled - 1 if rest == 0 and 1 <= scaled <= N_BLOCKS else None
+                full = scaled is not None and scaled == BATCHES[batch_of[scaled][0]][-1]
+                if full:
+                    sizes(batch_of[scaled][0])
                 if 0 <= step < N_UNITS:
                     if step % UNITS_PER_BLOCK == GPSIMD_QUARTER:
                         weigh_on_gpsimd(step)
                     else:
                         weigh(step)
+                if full:
+                    scale_and_store(batch_of[scaled][0])
                 done, rest = divmod(step, UNITS_PER_BLOCK)
                 if rest == 0 and 1 <= done <= N_BLOCKS:
                     quantise(done - 1)
                 closed, rest = divmod(step - MX_LAG + 1, UNITS_PER_BLOCK)
                 if rest == 0 and 1 <= closed <= N_BLOCKS:
-                    norms(closed - 1)
-                scaled, rest = divmod(step - MX_LAG - SCALE_LAG + 1, UNITS_PER_BLOCK)
-                if rest == 0 and 1 <= scaled <= N_BLOCKS:
-                    scale_and_store(scaled - 1)
+                    empty(closed - 1)

@@ -30,8 +30,8 @@ GROUP = 4
 GPSIMD_QUARTER = 0
 
 SCORE_LEAD = 1
-MX_LAG = 6
-SCALE_LAG = 3
+MX_LAG = 8
+SCALE_LAG = 5
 NORM_BATCH = 4
 BATCHES = [list(range(b, b + NORM_BATCH)) for b in range(0, N_BLOCKS - NORM_BATCH, NORM_BATCH)] + [
     [N_BLOCKS - 4, N_BLOCKS - 3],
@@ -63,7 +63,7 @@ def tile_hybonetconv_pb_t_kernel(tc, q_neg, k, h, adj, att_bias, att_scale, out)
         result_pool = ctx.enter_context(tc.tile_pool(name="result", bufs=4))
 
         h_sb = const.tile([P, N_PASS * PACK, D], BF16)
-        nc.sync.dma_start(out=h_sb[:].rearrange("p (g t) d -> p g (t d)", t=PACK), in_=h_view)
+        h_passes = h_sb[:].rearrange("p (g t) d -> p g (t d)", t=PACK)
         q_sb = const.tile([P, N_BLOCKS, D], BF16)
         nc.sync.dma_start(out=q_sb[:, 0:GROUP, :], in_=q_view[:, 0:GROUP, :])
         k_sb = const.tile([P, N_PASS * PACK, D], BF16)
@@ -76,6 +76,9 @@ def tile_hybonetconv_pb_t_kernel(tc, q_neg, k, h, adj, att_bias, att_scale, out)
             nc.sync.dma_start(out=k_passes[:, passes, :], in_=k_view[:, passes, :])
             cols = slice(UNIT_J * quarter, UNIT_J * (quarter + 1))
             nc.sync.dma_start(out=adj_tiles[0][:, cols], in_=adj_view[0][:, cols])
+            if quarter % 2 == 1:
+                half = slice(PASSES_PER_UNIT * (quarter - 1), PASSES_PER_UNIT * (quarter + 1))
+                nc.sync.dma_start(out=h_passes[:, half, :], in_=h_view[:, half, :])
 
         def load_adj(b):
             adj_sb = adj_pool.tile([P, N], BF16, name="adj_sb")
@@ -106,16 +109,27 @@ def tile_hybonetconv_pb_t_kernel(tc, q_neg, k, h, adj, att_bias, att_scale, out)
         nc.vector.tensor_add(out=sig_bias[:], in0=sig_scale[:], in1=bias_bf[:])
 
         h_grouped = const.tile([P, N_PASS, D, PACK], BF16, align_bytes=64)
-        nc.vector.tensor_copy(
-            out=h_grouped[:], in_=h_sb[:].rearrange("p (g t) d -> p g d t", t=PACK)
-        )
         h_words = const.tile([P, N_PASS, D], U32, align_bytes=64)
         h_scales = const.tile([P, N_PASS, D], U8, align_bytes=64)
-        nc.vector.quantize_mx(
-            out=h_words[:].rearrange("p g d -> p (g d)").bitcast(FP8X4),
-            scales=h_scales[:].rearrange("p g d -> p (g d)"),
-            in_=h_grouped[:].rearrange("p g d t -> p (g d t)"),
-        )
+
+        def regroup_h(half):
+            first = half * N_PASS // 2
+            for g in range(first, first + N_PASS // 2):
+                nc.gpsimd.tensor_scalar(
+                    out=h_grouped[:, g, :, :],
+                    in0=h_sb[:, PACK * g : PACK * (g + 1), :].rearrange("p t d -> p d t"),
+                    scalar1=1.0,
+                    scalar2=0.0,
+                    op0=ALU.mult,
+                    op1=ALU.add,
+                )
+
+        def quantise_h():
+            nc.vector.quantize_mx(
+                out=h_words[:].rearrange("p g d -> p (g d)").bitcast(FP8X4),
+                scales=h_scales[:].rearrange("p g d -> p (g d)"),
+                in_=h_grouped[:].rearrange("p g d t -> p (g d t)"),
+            )
 
         cin_ps = ctx.enter_context(tc.psum_pool(name="cin_ps", bufs=3))
         adjT_ps = ctx.enter_context(tc.psum_pool(name="adjT_ps", bufs=3))
@@ -124,11 +138,11 @@ def tile_hybonetconv_pb_t_kernel(tc, q_neg, k, h, adj, att_bias, att_scale, out)
         qT = const.tile([P, N_BLOCKS, P], BF16)
         kT = const.tile([P, N_PASS * PACK, P], BF16)
 
-        def turn(src, dst, first):
+        def turn(src, dst, first, copy):
             turned = cin_ps.tile([P, GROUP, P], BF16, name="turned", tag="cin")
             for n in range(GROUP):
                 nc.tensor.transpose(turned[:, n, :], src[:, first + n, :], ident_bf[:])
-            nc.scalar.copy(out=dst[:, first : first + GROUP, :], in_=turned[:])
+            copy(out=dst[:, first : first + GROUP, :], in_=turned[:])
 
         adjT_tiles = {}
         cin_tiles = {}
@@ -213,14 +227,17 @@ def tile_hybonetconv_pb_t_kernel(tc, q_neg, k, h, adj, att_bias, att_scale, out)
                     op=ALU.mult,
                 )
 
-        def quantise(b):
-            words = mx_pool.tile([P, N_PASS * P], U32, name="words", align_bytes=64)
-            planes = mx_pool.tile([P, N_PASS * P], U8, name="planes", align_bytes=64)
+        def quantise(b, quarters=range(UNITS_PER_BLOCK)):
+            if b not in word_tiles:
+                word_tiles[b] = mx_pool.tile([P, N_PASS * P], U32, name="words", align_bytes=64)
+                plane_tiles[b] = mx_pool.tile([P, N_PASS * P], U8, name="planes", align_bytes=64)
+            cols = slice(quarters.start * UNIT_COLS, quarters.stop * UNIT_COLS)
+            vals = slice(quarters.start * UNIT_VALS, quarters.stop * UNIT_VALS)
             nc.vector.quantize_mx(
-                out=words[:].bitcast(FP8X4), scales=planes[:], in_=att_tiles[b][:]
+                out=word_tiles[b][:, cols].bitcast(FP8X4),
+                scales=plane_tiles[b][:, cols],
+                in_=att_tiles[b][:, vals],
             )
-            word_tiles[b] = words
-            plane_tiles[b] = planes
 
         def aggregate(s):
             b, quarter = divmod(s, UNITS_PER_BLOCK)
@@ -282,9 +299,10 @@ def tile_hybonetconv_pb_t_kernel(tc, q_neg, k, h, adj, att_bias, att_scale, out)
             nc.gpsimd.tensor_tensor(
                 out=rnorm[:, 0:n], in0=floored_tiles[batch][:, 0:n], in1=minus_half[:, 0:n], op=ALU.pow
             )
+            scale = nc.gpsimd.tensor_scalar if batch < len(BATCHES) - 1 else nc.vector.tensor_scalar
             for j, b in enumerate(BATCHES[batch]):
                 result = result_pool.tile([P, D], F32, name="result")
-                nc.gpsimd.tensor_scalar(
+                scale(
                     out=result[:],
                     in0=support_sb_tiles[batch][:, j, :],
                     scalar1=rnorm[:, j : j + 1],
@@ -305,10 +323,11 @@ def tile_hybonetconv_pb_t_kernel(tc, q_neg, k, h, adj, att_bias, att_scale, out)
                 if ahead < N_UNITS:
                     b_ahead, quarter_ahead = divmod(ahead, UNITS_PER_BLOCK)
                     if quarter_ahead == 0 and b_ahead % GROUP == 0:
-                        turn(q_sb, qT, b_ahead)
+                        turn(q_sb, qT, b_ahead, nc.vector.tensor_copy if b_ahead == 0 else nc.scalar.copy)
                     if b_ahead == 0:
                         for gg in range(PASSES_PER_UNIT):
-                            turn(k_sb, kT, PACK * (PASSES_PER_UNIT * quarter_ahead + gg))
+                            copy = nc.scalar.copy if gg == 0 else nc.vector.tensor_copy
+                            turn(k_sb, kT, PACK * (PASSES_PER_UNIT * quarter_ahead + gg), copy)
                     scores(ahead, 0)
                 if 0 <= step - MX_LAG < N_UNITS:
                     aggregate(step - MX_LAG)
@@ -321,15 +340,23 @@ def tile_hybonetconv_pb_t_kernel(tc, q_neg, k, h, adj, att_bias, att_scale, out)
                 if full:
                     sizes(batch_of[scaled][0])
                 if 0 <= step < N_UNITS:
-                    if step % UNITS_PER_BLOCK == GPSIMD_QUARTER:
+                    if step % UNITS_PER_BLOCK == GPSIMD_QUARTER and step >= UNITS_PER_BLOCK:
                         weigh_on_gpsimd(step)
                     else:
                         weigh(step)
                 if full:
                     scale_and_store(batch_of[scaled][0])
                 done, rest = divmod(step, UNITS_PER_BLOCK)
-                if rest == 0 and 1 <= done <= N_BLOCKS:
+                if rest == 0 and 1 <= done < N_BLOCKS:
                     quantise(done - 1)
+                if step in (0, 1):
+                    regroup_h(step)
+                if step == UNITS_PER_BLOCK + 1:
+                    quantise_h()
+                if step == N_UNITS - 2:
+                    quantise(N_BLOCKS - 1, range(0, 2))
+                if step == N_UNITS:
+                    quantise(N_BLOCKS - 1, range(2, 4))
                 closed, rest = divmod(step - MX_LAG + 1, UNITS_PER_BLOCK)
                 if rest == 0 and 1 <= closed <= N_BLOCKS:
                     empty(closed - 1)

from contextlib import ExitStack

import concourse.masks as masks
import concourse.mybir as mybir

F32 = mybir.dt.float32
BF16 = mybir.dt.bfloat16
U32 = mybir.dt.uint32
U8 = mybir.dt.uint8
FP8X4 = mybir.dt.float8_e4m3fn_x4
FUNC = mybir.ActivationFunctionType
ALU = mybir.AluOpType

P = 128
N = 4096
D = 128
PACK = 4
K_PASS = P * PACK
N_PASS = N // K_PASS
N_BLOCKS = N // P

PASSES_PER_UNIT = 2
UNITS_PER_BLOCK = N_PASS // PASSES_PER_UNIT
N_UNITS = N_BLOCKS * UNITS_PER_BLOCK
UNIT_COLS = PASSES_PER_UNIT * P
UNIT_VALS = UNIT_COLS * PACK
UNIT_J = PASSES_PER_UNIT * K_PASS
GROUP = 4

GPSIMD_QUARTER = 0

SCORE_LEAD = 1
MX_LAG = 8
SCALE_LAG = 5
NORM_BATCH = 4
BATCHES = [list(range(b, b + NORM_BATCH)) for b in range(0, N_BLOCKS - NORM_BATCH, NORM_BATCH)] + [
    [N_BLOCKS - 4, N_BLOCKS - 3],
    [N_BLOCKS - 2],
    [N_BLOCKS - 1],
]
ADJ_AHEAD = 4

FLOPS = 2 * (2 * N * N * D)


def tile_hybonetconv_pb_t_kernel(tc, q_neg, k, h, adj, att_bias, att_scale, out):
    nc = tc.nc

    q_view = q_neg.rearrange("(p b) d -> p b d", b=N_BLOCKS)
    adj_view = adj.rearrange("(p b) j -> b p j", b=N_BLOCKS)
    out_view = out.rearrange("(p b) d -> p b d", b=N_BLOCKS)
    k_view = k.rearrange("(g p t) d -> p g (t d)", p=P, t=PACK)
    h_view = h.rearrange("(g p t) d -> p g (t d)", p=P, t=PACK)

    with ExitStack() as ctx:
        const = ctx.enter_context(tc.tile_pool(name="const", bufs=1))
        adj_pool = ctx.enter_context(tc.tile_pool(name="adj", bufs=ADJ_AHEAD + 1))
        sig_pool = ctx.enter_context(tc.tile_pool(name="sig", bufs=6 + SCORE_LEAD))
        att_pool = ctx.enter_context(tc.tile_pool(name="att", bufs=3))
        mx_pool = ctx.enter_context(tc.tile_pool(name="mx", bufs=3))
        side_pool = ctx.enter_context(tc.tile_pool(name="side", bufs=2))
        norm_pool = ctx.enter_context(tc.tile_pool(name="norm", bufs=2))
        result_pool = ctx.enter_context(tc.tile_pool(name="result", bufs=4))

        h_sb = const.tile([P, N_PASS * PACK, D], BF16)
        h_passes = h_sb[:].rearrange("p (g t) d -> p g (t d)", t=PACK)
        q_sb = const.tile([P, N_BLOCKS, D], BF16)
        nc.sync.dma_start(out=q_sb[:, 0:GROUP, :], in_=q_view[:, 0:GROUP, :])
        k_sb = const.tile([P, N_PASS * PACK, D], BF16)
        k_passes = k_sb[:].rearrange("p (g t) d -> p g (t d)", t=PACK)

        adj_tiles = {}
        adj_tiles[0] = adj_pool.tile([P, N], BF16, name="adj_sb")
        for quarter in range(UNITS_PER_BLOCK):
            passes = slice(PASSES_PER_UNIT * quarter, PASSES_PER_UNIT * (quarter + 1))
            nc.sync.dma_start(out=k_passes[:, passes, :], in_=k_view[:, passes, :])
            cols = slice(UNIT_J * quarter, UNIT_J * (quarter + 1))
            nc.sync.dma_start(out=adj_tiles[0][:, cols], in_=adj_view[0][:, cols])
            if quarter % 2 == 1:
                half = slice(PASSES_PER_UNIT * (quarter - 1), PASSES_PER_UNIT * (quarter + 1))
                nc.sync.dma_start(out=h_passes[:, half, :], in_=h_view[:, half, :])

        def load_adj(b):
            adj_sb = adj_pool.tile([P, N], BF16, name="adj_sb")
            nc.sync.dma_start(out=adj_sb[:], in_=adj_view[b])
            adj_tiles[b] = adj_sb

        load_adj(1)
        load_adj(2)
        nc.sync.dma_start(out=q_sb[:, GROUP:N_BLOCKS, :], in_=q_view[:, GROUP:N_BLOCKS, :])
        load_adj(3)

        scale_bf = const.tile([P, 1], BF16)
        nc.scalar.dma_start(out=scale_bf[:], in_=att_scale.partition_broadcast(P))
        bias_bf = const.tile([P, 1], BF16)
        nc.scalar.dma_start(out=bias_bf[:], in_=att_bias.partition_broadcast(P))

        ident_bf = const.tile([P, P], BF16)
        masks.make_identity(nc, ident_bf[:])
        ident_f32 = const.tile([P, P], F32)
        masks.make_identity(nc, ident_f32[:])
        minus_half = const.tile([P, NORM_BATCH], F32)
        nc.gpsimd.memset(minus_half[:], -0.5)

        sig_scale = const.tile([P, 1], F32)
        nc.vector.reciprocal(out=sig_scale[:], in_=scale_bf[:])
        nc.vector.tensor_scalar_mul(out=sig_scale[:], in0=sig_scale[:], scalar1=2.0)
        sig_bias = const.tile([P, 1], F32)
        nc.vector.tensor_add(out=sig_bias[:], in0=sig_scale[:], in1=bias_bf[:])

        h_grouped = const.tile([P, N_PASS, D, PACK], BF16, align_bytes=64)
        h_words = const.tile([P, N_PASS, D], U32, align_bytes=64)
        h_scales = const.tile([P, N_PASS, D], U8, align_bytes=64)

        def regroup_h(half):
            first = half * N_PASS // 2
            for g in range(first, first + N_PASS // 2):
                nc.gpsimd.tensor_scalar(
                    out=h_grouped[:, g, :, :],
                    in0=h_sb[:, PACK * g : PACK * (g + 1), :].rearrange("p t d -> p d t"),
                    scalar1=1.0,
                    scalar2=0.0,
                    op0=ALU.mult,
                    op1=ALU.add,
                )

        def quantise_h():
            nc.vector.quantize_mx(
                out=h_words[:].rearrange("p g d -> p (g d)").bitcast(FP8X4),
                scales=h_scales[:].rearrange("p g d -> p (g d)"),
                in_=h_grouped[:].rearrange("p g d t -> p (g d t)"),
            )

        cin_ps = ctx.enter_context(tc.psum_pool(name="cin_ps", bufs=3))
        adjT_ps = ctx.enter_context(tc.psum_pool(name="adjT_ps", bufs=3))
        sup_ps = ctx.enter_context(tc.psum_pool(name="sup_ps", bufs=2))

        qT = const.tile([P, N_BLOCKS, P], BF16)
        kT = const.tile([P, N_PASS * PACK, P], BF16)

        def turn(src, dst, first, copy):
            turned = cin_ps.tile([P, GROUP, P], BF16, name="turned", tag="cin")
            for n in range(GROUP):
                nc.tensor.transpose(turned[:, n, :], src[:, first + n, :], ident_bf[:])
            copy(out=dst[:, first : first + GROUP, :], in_=turned[:])

        adjT_tiles = {}
        cin_tiles = {}
        sig_tiles = {}
        att_tiles = {}
        word_tiles = {}
        plane_tiles = {}
        support_tiles = {}
        squares_tiles = {}
        total_tiles = {}
        support_sb_tiles = {}
        floored_tiles = {}
        batch_of = {b: (batch, j) for batch, blocks in enumerate(BATCHES) for j, b in enumerate(blocks)}

        def transpose_adj(s):
            b, quarter = divmod(s, UNITS_PER_BLOCK)
            adj_words = adj_tiles[b][:].bitcast(F32)
            adjT = adjT_ps.tile([P, 2, PASSES_PER_UNIT, P], F32, name="adjT")
            for gg in range(PASSES_PER_UNIT):
                for u in range(2):
                    first = 2 * P * (PASSES_PER_UNIT * quarter + gg)
                    nc.tensor.transpose(
                        adjT[:, u, gg, :], adj_words[:, first + u : first + 2 * P : 2], ident_f32[:]
                    )
            adjT_tiles[s] = adjT

        def scores(s, gg):
            b, quarter = divmod(s, UNITS_PER_BLOCK)
            g = PASSES_PER_UNIT * quarter + gg
            cin = cin_ps.tile([P, PACK, P], F32, name="cin", tag="cin")
            for t in range(PACK):
                nc.tensor.matmul(
                    out=cin[:, t, :],
                    lhsT=kT[:, PACK * g + t, :],
                    rhs=qT[:, b, :],
                    start=True,
                    stop=True,
                )
            cin_tiles[(s, gg)] = cin

        def sigmoid(s):
            sig = sig_pool.tile([P, UNIT_VALS], F32, name="sig")
            for gg in range(PASSES_PER_UNIT):
                nc.scalar.activation(
                    out=sig[:, gg * K_PASS : (gg + 1) * K_PASS].rearrange(
                        "p (i t) -> p i t", t=PACK
                    ),
                    in_=cin_tiles[(s, gg)][:].rearrange("p t i -> p i t"),
                    func=FUNC.Sigmoid,
                    bias=sig_bias[:],
                    scale=sig_scale[:],
                )
            sig_tiles[s] = sig

        def att_of(s):
            b, quarter = divmod(s, UNITS_PER_BLOCK)
            if b not in att_tiles:
                att_tiles[b] = att_pool.tile([P, UNITS_PER_BLOCK * UNIT_VALS], BF16, name="att", align_bytes=64)
            return att_tiles[b][:, quarter * UNIT_VALS : (quarter + 1) * UNIT_VALS]

        def weigh(s):
            adjT_bf = adjT_tiles[s][:].rearrange("p u gg i -> p (u gg i)").bitcast(BF16)
            nc.vector.tensor_tensor(
                out=att_of(s).rearrange("p (c u e) -> p c u e", u=2, e=2),
                in0=sig_tiles[s][:].rearrange("p (c u e) -> p c u e", u=2, e=2),
                in1=adjT_bf.rearrange("p (u c e) -> p c u e", u=2, e=2),
                op=ALU.mult,
            )

        def weigh_on_gpsimd(s):
            adjS = side_pool.tile([P, UNIT_COLS, 2], F32, name="adjS")
            nc.vector.tensor_copy(
                out=adjS[:], in_=adjT_tiles[s][:].rearrange("p u gg i -> p (gg i) u")
            )
            adjS_bf = adjS[:].rearrange("p c u -> p (c u)").bitcast(BF16)
            for gg in range(PASSES_PER_UNIT):
                vals = slice(gg * K_PASS, (gg + 1) * K_PASS)
                nc.gpsimd.tensor_tensor(
                    out=att_of(s)[:, vals],
                    in0=sig_tiles[s][:, vals],
                    in1=adjS_bf[:, vals],
                    op=ALU.mult,
                )

        def quantise(b, quarters=range(UNITS_PER_BLOCK)):
            if b not in word_tiles:
                word_tiles[b] = mx_pool.tile([P, N_PASS * P], U32, name="words", align_bytes=64)
                plane_tiles[b] = mx_pool.tile([P, N_PASS * P], U8, name="planes", align_bytes=64)
            cols = slice(quarters.start * UNIT_COLS, quarters.stop * UNIT_COLS)
            vals = slice(quarters.start * UNIT_VALS, quarters.stop * UNIT_VALS)
            nc.vector.quantize_mx(
                out=word_tiles[b][:, cols].bitcast(FP8X4),
                scales=plane_tiles[b][:, cols],
                in_=att_tiles[b][:, vals],
            )

        def aggregate(s):
            b, quarter = divmod(s, UNITS_PER_BLOCK)
            if quarter == 0:
                support_tiles[b] = sup_ps.tile([P, D], F32, name="support")
            words = word_tiles[b]
            planes = plane_tiles[b]
            for gg in range(PASSES_PER_UNIT):
                g = PASSES_PER_UNIT * quarter + gg
                cols = slice(g * P, (g + 1) * P)
                nc.tensor.matmul_mx(
                    out=support_tiles[b][:],
                    lhsT=words[:, cols].bitcast(FP8X4),
                    lhsT_scale=planes[:, cols],
                    rhs=h_words[:, g, :].bitcast(FP8X4),
                    rhs_scale=h_scales[:, g, :],
                    start=(g == 0),
                    stop=(g == N_PASS - 1),
                )

        def empty(b):
            batch, j = batch_of[b]
            if j == 0:
                squares_tiles[batch] = norm_pool.tile([P, NORM_BATCH, D], F32, name="squares")
                total_tiles[batch] = norm_pool.tile([P, NORM_BATCH], F32, name="total")
                support_sb_tiles[batch] = norm_pool.tile([P, NORM_BATCH, D], F32, name="support_sb")
            nc.scalar.activation(
                out=squares_tiles[batch][:, j, :],
                in_=support_tiles[b][:],
                func=FUNC.Square,
                accum_out=total_tiles[batch][:, j : j + 1],
            )
            nc.scalar.copy(out=support_sb_tiles[batch][:, j, :], in_=support_tiles[b][:])

        def sizes(batch):
            n = len(BATCHES[batch])
            lorentz = norm_pool.tile([P, NORM_BATCH], F32, name="lorentz")
            nc.vector.scalar_tensor_tensor(
                out=lorentz[:, 0:n],
                in0=squares_tiles[batch][:, 0:n, 0],
                scalar=-2.0,
                in1=total_tiles[batch][:, 0:n],
                op0=ALU.mult,
                op1=ALU.add,
            )
            size = norm_pool.tile([P, NORM_BATCH], F32, name="size")
            nc.vector.scalar_tensor_tensor(
                out=size[:, 0:n], in0=lorentz[:, 0:n], scalar=-1.0, in1=lorentz[:, 0:n], op0=ALU.mult, op1=ALU.max
            )
            floored = norm_pool.tile([P, NORM_BATCH], F32, name="floored")
            nc.vector.tensor_scalar(
                out=floored[:, 0:n], in0=size[:, 0:n], scalar1=1e-6, scalar2=None, op0=ALU.max
            )
            floored_tiles[batch] = floored

        def scale_and_store(batch):
            n = len(BATCHES[batch])
            rnorm = norm_pool.tile([P, NORM_BATCH], F32, name="rnorm")
            nc.gpsimd.tensor_tensor(
                out=rnorm[:, 0:n], in0=floored_tiles[batch][:, 0:n], in1=minus_half[:, 0:n], op=ALU.pow
            )
            scale = nc.gpsimd.tensor_scalar if batch < len(BATCHES) - 1 else nc.vector.tensor_scalar
            for j, b in enumerate(BATCHES[batch]):
                result = result_pool.tile([P, D], F32, name="result")
                scale(
                    out=result[:],
                    in0=support_sb_tiles[batch][:, j, :],
                    scalar1=rnorm[:, j : j + 1],
                    scalar2=0.0,
                    op0=ALU.mult,
                    op1=ALU.add,
                )
                nc.sync.dma_start(out=out_view[:, b, :], in_=result[:])

        with tc.manual_schedule():
            for step in range(-SCORE_LEAD, N_UNITS + MX_LAG + SCALE_LAG):
                ahead = step + SCORE_LEAD
                if 0 <= step < N_UNITS:
                    b, quarter = divmod(step, UNITS_PER_BLOCK)
                    if quarter == 0 and b + ADJ_AHEAD < N_BLOCKS:
                        load_adj(b + ADJ_AHEAD)
                    transpose_adj(step)
                if ahead < N_UNITS:
                    b_ahead, quarter_ahead = divmod(ahead, UNITS_PER_BLOCK)
                    if quarter_ahead == 0 and b_ahead % GROUP == 0:
                        turn(q_sb, qT, b_ahead, nc.vector.tensor_copy if b_ahead == 0 else nc.scalar.copy)
                    if b_ahead == 0:
                        for gg in range(PASSES_PER_UNIT):
                            copy = nc.scalar.copy if gg == 0 else nc.vector.tensor_copy
                            turn(k_sb, kT, PACK * (PASSES_PER_UNIT * quarter_ahead + gg), copy)
                    scores(ahead, 0)
                if 0 <= step - MX_LAG < N_UNITS:
                    aggregate(step - MX_LAG)
                if ahead < N_UNITS:
                    scores(ahead, 1)
                    sigmoid(ahead)
                scaled, rest = divmod(step - MX_LAG - SCALE_LAG + 1, UNITS_PER_BLOCK)
                scaled = scaled - 1 if rest == 0 and 1 <= scaled <= N_BLOCKS else None
                full = scaled is not None and scaled == BATCHES[batch_of[scaled][0]][-1]
                if full:
                    sizes(batch_of[scaled][0])
                if 0 <= step < N_UNITS:
                    if step % UNITS_PER_BLOCK == GPSIMD_QUARTER and step >= UNITS_PER_BLOCK:
                        weigh_on_gpsimd(step)
                    else:
                        weigh(step)
                if full:
                    scale_and_store(batch_of[scaled][0])
                done, rest = divmod(step, UNITS_PER_BLOCK)
                if rest == 0 and 1 <= done < N_BLOCKS:
                    quantise(done - 1)
                if step in (0, 1):
                    regroup_h(step)
                if step == UNITS_PER_BLOCK + 1:
                    quantise_h()
                if step == N_UNITS - 2:
                    quantise(N_BLOCKS - 1, range(0, 2))
                if step == N_UNITS:
                    quantise(N_BLOCKS - 1, range(2, 4))
                closed, rest = divmod(step - MX_LAG + 1, UNITS_PER_BLOCK)
                if rest == 0 and 1 <= closed <= N_BLOCKS:
                    empty(closed - 1)
